import numpy as np
import ml_dtypes


def mxq(x, axis, fmt="e4m3"):
    dtype, down = {"e4m3": (ml_dtypes.float8_e4m3fn, 7), "e5m2": (ml_dtypes.float8_e5m2, 14)}[fmt]
    v = np.moveaxis(np.asarray(x, np.float32).astype(ml_dtypes.bfloat16).astype(np.float64), axis, -1)
    blocks = v.reshape(v.shape[:-1] + (-1, 32))
    amax = np.abs(blocks).max(-1, keepdims=True)
    byte = np.maximum(np.where(amax > 0, np.frexp(amax)[1] - 1 + 127, 0) - down, 1)
    scale = np.exp2(byte - 127.0)
    codes = (blocks / scale).astype(np.float32).astype(dtype).astype(np.float64)
    return np.moveaxis((codes * scale).reshape(v.shape), -1, axis)


WIDE = False


def mx_kscale(k):
    if not WIDE:
        return np.ones(k)
    levels = np.array([10, -10, 5, -5, 0])
    a = np.random.permutation(np.resize(levels, k // 512 * 4)).reshape(k // 512, 4)
    idx = np.arange(k)
    return np.exp2(a[idx // 512, idx % 128 // 32])


BF16 = ml_dtypes.bfloat16


def bf(x):
    return np.asarray(x, np.float32).astype(BF16)


def f64(x):
    return np.asarray(x).astype(np.float64)


E2M1 = np.array([0.0, 0.5, 1.0, 1.5, 2.0, 3.0, 4.0, 6.0, -0.0, -0.5, -1.0, -1.5, -2.0, -3.0, -4.0, -6.0])


def pack_weight(w, fmt):
    k, n = w.shape
    w = f64(bf(w)).reshape(k // 32, 32, n)
    amax = np.abs(w).max(1)
    if fmt == "e4m3":
        byte = np.frexp(amax)[1] - 1 + 127 - 7
    else:
        mant, ex = np.frexp(amax / 6.0)
        byte = np.where(mant > 0.5, ex, ex - 1) + 127
    byte = np.clip(np.where(amax > 0, byte, 1), 1, 254)
    scaled = (w * np.exp2(127.0 - byte)[:, None, :]).reshape(k, n).astype(np.float32)
    by_word = np.ascontiguousarray(scaled.reshape(k // 512, 128, 4, n).transpose(0, 1, 3, 2))
    if fmt == "e4m3":
        words = by_word.astype(ml_dtypes.float8_e4m3fn).view(np.uint8)
    else:
        c = by_word.astype(ml_dtypes.float4_e2m1fn).view(np.uint8) & 0xF
        words = c[..., 0::2] | (c[..., 1::2] << 4)
    return np.ascontiguousarray(words), np.ascontiguousarray(byte.astype(np.uint8).reshape(k // 512, 16, n))


def unpack_weight(words, scales, fmt):
    g, p, n, _ = words.shape
    if fmt == "e4m3":
        vals = np.ascontiguousarray(words).view(ml_dtypes.float8_e4m3fn).astype(np.float64)
    else:
        nib = np.empty((g, p, n, 4), np.uint8)
        nib[..., 0::2] = words & 0xF
        nib[..., 1::2] = words >> 4
        vals = E2M1[nib]
    vals = vals * np.repeat(np.exp2(scales.astype(np.float64) - 127.0), 8, axis=1)[..., None]
    return vals.transpose(0, 1, 3, 2).reshape(g * 512, n)


B, T, D, H = 1, 384, 2048, 16
HD = D // H
ROPE_BASE = 10000.0
FMT = "e4m3"


def rope_table():
    theta = 1.0 / (ROPE_BASE ** (np.arange(0, HD, 2) / HD))
    angles = np.arange(T)[:, None] * theta[None, :]
    return np.stack([np.cos(angles), np.sin(angles)], axis=-1)


def apply_rotary_emb(v, f_tab):
    vr = v.reshape(*v.shape[:-1], -1, 2)
    f = f_tab[None, :, None, :, :]
    v0, v1 = vr[..., 0], vr[..., 1]
    f0, f1 = f[..., 0], f[..., 1]
    y = np.stack([v0 * f0 - v1 * f1, v0 * f1 + v1 * f0], axis=-1)
    return y.reshape(v.shape)


def setup_inputs():
    s = mx_kscale(D)
    x = bf(np.random.standard_normal((B, T, D)) * s)
    freqs_cis = bf(rope_table())
    wq = np.random.standard_normal((D, D)) * 1.5 / np.sqrt(D) / s[None, :]
    wk = np.random.standard_normal((D, D)) * 1.5 / np.sqrt(D) / s[None, :]
    wv = np.random.standard_normal((D, D)) * 1.0 / np.sqrt(D) / s[None, :]
    wq_words, wq_scales = pack_weight(wq.T, FMT)
    wk_words, wk_scales = pack_weight(wk.T, FMT)
    wv_words, wv_scales = pack_weight(wv.T, FMT)
    return {"x": x,
            "freqs_cis": freqs_cis,
            "wq_words": wq_words, "wq_scales": wq_scales,
            "wk_words": wk_words, "wk_scales": wk_scales,
            "wv_words": wv_words, "wv_scales": wv_scales}


def reference(x, freqs_cis, wq_words, wq_scales, wk_words, wk_scales, wv_words, wv_scales):
    xm = mxq(f64(x), 2, "e4m3")
    q = (xm @ unpack_weight(wq_words, wq_scales, FMT)).reshape(B, T, H, HD)
    k = (xm @ unpack_weight(wk_words, wk_scales, FMT)).reshape(B, T, H, HD)
    v = (xm @ unpack_weight(wv_words, wv_scales, FMT)).reshape(B, T, H, HD)
    f_tab = f64(freqs_cis)
    return apply_rotary_emb(q, f_tab), apply_rotary_emb(k, f_tab), v

@@ -1,0 +1,164 @@
+from contextlib import ExitStack
+
+import concourse.masks as masks
+import concourse.mybir as mybir
+
+F32 = mybir.dt.float32
+BF16 = mybir.dt.bfloat16
+I32 = mybir.dt.int32
+U32 = mybir.dt.uint32
+U8 = mybir.dt.uint8
+FP8X4 = mybir.dt.float8_e4m3fn_x4
+MULT = mybir.AluOpType.mult
+ADD = mybir.AluOpType.add
+
+P = 128
+TOKENS = 384
+FEATURES = 2048
+HEAD = 128
+PAIRS = HEAD // 2
+TOKEN_TILES = TOKENS // P
+PACK = 4
+K_PASS = P * PACK
+PASSES = FEATURES // K_PASS
+BANK = 512
+HALF = 1024
+BANKS_PER_HALF = HALF // BANK
+HALVES = FEATURES // HALF
+HEADS_PER_BANK = BANK // HEAD
+WEIGHTS = 3
+ROTATED = 2
+QUADRANTS = 4
+PLANE_ROWS = 4
+
+FLOPS = 2 * TOKENS * FEATURES * WEIGHTS * FEATURES
+
+
+def load_scale_planes(nc, planes, scales):
+    for quadrant in range(QUADRANTS):
+        first = 32 * quadrant
+        rows = slice(PLANE_ROWS * quadrant, PLANE_ROWS * (quadrant + 1))
+        nc.sync.dma_start(
+            out=planes[first : first + PASSES * PLANE_ROWS, :].bitcast(I32),
+            in_=scales[:, rows, :].bitcast(I32),
+        )
+
+
+def rotate(nc, scratch, acc, y, cos_m, sin_m):
+    by_head = [P, HEADS_PER_BANK, HEAD]
+    by_pair = [P, HEADS_PER_BANK, PAIRS, 2]
+    nc.vector.tensor_tensor(
+        out=y.rearrange("p (h d) -> p h d", d=HEAD),
+        in0=acc[:].rearrange("p (h d) -> p h d", d=HEAD),
+        in1=cos_m.unsqueeze(1).to_broadcast(by_head),
+        op=MULT,
+    )
+    crossed = scratch.tile([P, BANK], F32)
+    nc.vector.tensor_tensor(
+        out=crossed[:].rearrange("p (h j e) -> p h j e", j=PAIRS, e=2),
+        in0=acc[:].rearrange("p (h j e) -> p h j e", j=PAIRS, e=2)[:, :, :, ::-1],
+        in1=sin_m.rearrange("p (j e) -> p j e", e=2).unsqueeze(1).to_broadcast(by_pair),
+        op=MULT,
+    )
+    nc.gpsimd.tensor_tensor(out=y, in0=y, in1=crossed[:], op=ADD)
+
+
+def tile_attention_pa_kernel(
+    tc, x, freqs_cis, wq_words, wq_scales, wk_words, wk_scales, wv_words, wv_scales, out_0, out_1, out_2
+):
+    nc = tc.nc
+    x_tiles = x.rearrange("b (m p) k -> (b m) p k", p=P)
+    w_words = [w.rearrange("g p n t -> p g (n t)").bitcast(I32) for w in (wq_words, wk_words, wv_words)]
+    w_scales = [wq_scales, wk_scales, wv_scales]
+    outs = [o.rearrange("b (m p) h d -> (b m) p (h d)", p=P) for o in (out_0, out_1, out_2)]
+
+    with ExitStack() as ctx:
+        keep = ctx.enter_context(tc.tile_pool(name="keep", bufs=1))
+        scratch = ctx.enter_context(tc.tile_pool(name="scratch", bufs=6))
+        psum = ctx.enter_context(tc.psum_pool(name="psum", bufs=8))
+
+        x_raw = keep.tile([P, TOKEN_TILES, FEATURES], BF16)
+        table = keep.tile([P, TOKEN_TILES, HEAD], BF16)
+        w_planes = keep.tile([P, WEIGHTS, FEATURES], U8, align_bytes=64)
+        w_codes = [
+            [keep.tile([P, PASSES, HALF], U32, name="w_codes_%d_%d" % (w, h), align_bytes=64) for h in range(HALVES)]
+            for w in range(WEIGHTS)
+        ]
+
+        nc.vector.memset(w_planes[:].rearrange("p w n -> p (w n)").bitcast(I32), 0)
+
+        nc.scalar.dma_start(out=table[:], in_=freqs_cis.rearrange("(m p) j e -> p m (j e)", p=P))
+        for m in range(TOKEN_TILES):
+            nc.sync.dma_start(out=x_raw[:, m, :], in_=x_tiles[m])
+        for w in range(WEIGHTS):
+            load_scale_planes(nc, w_planes[:, w, :], w_scales[w])
+            for h in range(HALVES):
+                pieces = BANKS_PER_HALF if (w == 0 and h == 0) else 1
+                width = HALF // pieces
+                for piece in range(pieces):
+                    nc.sync.dma_start(
+                        out=w_codes[w][h][:, :, piece * width : (piece + 1) * width].bitcast(I32),
+                        in_=w_words[w][:, :, h * HALF + piece * width : h * HALF + (piece + 1) * width],
+                    )
+
+        cos_tab = keep.tile([P, TOKEN_TILES, HEAD], F32)
+        sin_tab = keep.tile([P, TOKEN_TILES, HEAD], F32)
+        table_pairs = table[:].rearrange("p m (j e) -> p (m j) e", e=2)
+        cos_pairs = cos_tab[:].rearrange("p m (j e) -> p (m j) e", e=2)
+        sin_pairs = sin_tab[:].rearrange("p m (j e) -> p (m j) e", e=2)
+        nc.scalar.copy(out=cos_pairs, in_=table_pairs[:, :, 0:1].to_broadcast([P, TOKEN_TILES * PAIRS, 2]))
+        nc.scalar.mul(out=sin_pairs[:, :, 0:1], in_=table_pairs[:, :, 1:2], mul=-1.0)
+        nc.scalar.copy(out=sin_pairs[:, :, 1:2], in_=table_pairs[:, :, 1:2])
+
+        identity = keep.tile([P, P], F32)
+        masks.make_identity(nc, identity[:])
+        x_grouped = keep.tile([P, TOKEN_TILES, PASSES * P * PACK], BF16, align_bytes=64)
+        x_codes = keep.tile([P, TOKEN_TILES, PASSES * P], U32, align_bytes=64)
+        x_planes = keep.tile([P, TOKEN_TILES, PASSES * P], U8, align_bytes=64)
+        passes_per_bank = BANK // (2 * P)
+        for m in range(TOKEN_TILES):
+            x_words = x_raw[:, m, :].bitcast(F32)
+            grouped_words = x_grouped[:, m, :].bitcast(F32)
+            for bank in range(PASSES // passes_per_bank):
+                turned = psum.tile([P, passes_per_bank, 2, P], F32, tag="bank")
+                for i in range(passes_per_bank):
+                    g = bank * passes_per_bank + i
+                    for u in range(2):
+                        nc.tensor.transpose(
+                            turned[:, i, u, :], x_words[:, 2 * P * g + u : 2 * P * (g + 1) : 2], identity[:]
+                        )
+                copy = nc.vector.tensor_copy if bank % 2 == 0 else nc.scalar.copy
+                copy(
+                    out=grouped_words[:, bank * BANK : (bank + 1) * BANK].rearrange(
+                        "p (i r u) -> p i r u", i=passes_per_bank, u=2
+                    ),
+                    in_=turned[:].rearrange("p i u r -> p i r u"),
+                )
+            nc.vector.quantize_mx(
+                out=x_codes[:, m, :].bitcast(FP8X4), scales=x_planes[:, m, :], in_=x_grouped[:, m, :]
+            )
+
+        for w in range(WEIGHTS):
+            for h in range(HALVES):
+                y_tiles = [keep.tile([P, HALF], F32, name="y_%d_%d_%d" % (w, h, m)) for m in range(TOKEN_TILES)]
+                for b in range(BANKS_PER_HALF):
+                    columns = slice(b * BANK, (b + 1) * BANK)
+                    for m in range(TOKEN_TILES):
+                        acc = psum.tile([P, BANK], F32, tag="bank")
+                        for g in range(PASSES):
+                            tokens = slice(g * P, (g + 1) * P)
+                            nc.tensor.matmul_mx(
+                                out=acc[:],
+                                lhsT=x_codes[:, m, tokens].bitcast(FP8X4),
+                                lhsT_scale=x_planes[:, m, tokens],
+                                rhs=w_codes[w][h][:, g, columns].bitcast(FP8X4),
+                                rhs_scale=w_planes[PLANE_ROWS * g : P, w, h * HALF + b * BANK : h * HALF + (b + 1) * BANK],
+                                start=(g == 0),
+                                stop=(g == PASSES - 1),
+                            )
+                        if w < ROTATED:
+                            rotate(nc, scratch, acc, y_tiles[m][:, columns], cos_tab[:, m, :], sin_tab[:, m, :])
+                        else:
+                            nc.scalar.copy(out=y_tiles[m][:, columns], in_=acc[:])
+                for m in range(TOKEN_TILES):
+                    nc.sync.dma_start(out=outs[w][m][:, h * HALF : (h + 1) * HALF], in_=y_tiles[m][:])

@@ -71,6 +71,7 @@ def tile_attention_pa_kernel(
     w_words = [w.rearrange("g p n t -> p g (n t)").bitcast(I32) for w in (wq_words, wk_words, wv_words)]
     w_scales = [wq_scales, wk_scales, wv_scales]
     outs = [o.rearrange("b (m p) h d -> (b m) p (h d)", p=P) for o in (out_0, out_1, out_2)]
+    banks = FEATURES // BANK
 
     with ExitStack() as ctx:
         keep = ctx.enter_context(tc.tile_pool(name="keep", bufs=1))
@@ -80,26 +81,29 @@ def tile_attention_pa_kernel(
         x_raw = keep.tile([P, TOKEN_TILES, FEATURES], BF16)
         table = keep.tile([P, TOKEN_TILES, HEAD], BF16)
         w_planes = keep.tile([P, WEIGHTS, FEATURES], U8, align_bytes=64)
-        w_codes = [
-            [keep.tile([P, PASSES, HALF], U32, name="w_codes_%d_%d" % (w, h), align_bytes=64) for h in range(HALVES)]
-            for w in range(WEIGHTS)
-        ]
 
         nc.vector.memset(w_planes[:].rearrange("p w n -> p (w n)").bitcast(I32), 0)
 
         nc.scalar.dma_start(out=table[:], in_=freqs_cis.rearrange("(m p) j e -> p m (j e)", p=P))
         for m in range(TOKEN_TILES):
             nc.sync.dma_start(out=x_raw[:, m, :], in_=x_tiles[m])
+
+        moving = [[[None] * banks for g in range(PASSES)] for w in range(WEIGHTS)]
         for w in range(WEIGHTS):
             load_scale_planes(nc, w_planes[:, w, :], w_scales[w])
-            for h in range(HALVES):
-                pieces = BANKS_PER_HALF if (w == 0 and h == 0) else 1
-                width = HALF // pieces
-                for piece in range(pieces):
-                    nc.sync.dma_start(
-                        out=w_codes[w][h][:, :, piece * width : (piece + 1) * width].bitcast(I32),
-                        in_=w_words[w][:, :, h * HALF + piece * width : h * HALF + (piece + 1) * width],
-                    )
+            if w == 0:
+                for first, width in ((0, BANK), (BANK, BANK), (HALF, HALF)):
+                    piece = keep.tile([P, PASSES, width], U32, name="wq_codes_%d" % first, align_bytes=64)
+                    nc.sync.dma_start(out=piece[:].bitcast(I32), in_=w_words[w][:, :, first : first + width])
+                    for g in range(PASSES):
+                        for b in range(width // BANK):
+                            moving[w][g][first // BANK + b] = piece[:, g, b * BANK : (b + 1) * BANK]
+            else:
+                for g in range(PASSES):
+                    rows = keep.tile([P, FEATURES], U32, name="w_codes_%d_%d" % (w, g), align_bytes=64)
+                    nc.sync.dma_start(out=rows[:].bitcast(I32), in_=w_words[w][:, g, :])
+                    for b in range(banks):
+                        moving[w][g][b] = rows[:, b * BANK : (b + 1) * BANK]
 
         cos_tab = keep.tile([P, TOKEN_TILES, HEAD], F32)
         sin_tab = keep.tile([P, TOKEN_TILES, HEAD], F32)
@@ -138,27 +142,40 @@ def tile_attention_pa_kernel(
                 out=x_codes[:, m, :].bitcast(FP8X4), scales=x_planes[:, m, :], in_=x_grouped[:, m, :]
             )
 
+        rounds_of = [
+            [[(m, b)] for b in range(banks) for m in range(TOKEN_TILES)],
+            [[(m, b) for m in range(TOKEN_TILES)] for b in range(banks)],
+            [[(m, b)] for m in range(TOKEN_TILES) for b in range(banks)],
+        ]
         for w in range(WEIGHTS):
-            for h in range(HALVES):
-                y_tiles = [keep.tile([P, HALF], F32, name="y_%d_%d_%d" % (w, h, m)) for m in range(TOKEN_TILES)]
-                for b in range(BANKS_PER_HALF):
+            y_tiles = [keep.tile([P, FEATURES], F32, name="y_%d_%d" % (w, m)) for m in range(TOKEN_TILES)]
+            for groups in rounds_of[w]:
+                accs = [psum.tile([P, BANK], F32, tag="bank", name="acc") for group in groups]
+                for g in range(PASSES):
+                    tokens = slice(g * P, (g + 1) * P)
+                    for (m, b), acc in zip(groups, accs):
+                        nc.tensor.matmul_mx(
+                            out=acc[:],
+                            lhsT=x_codes[:, m, tokens].bitcast(FP8X4),
+                            lhsT_scale=x_planes[:, m, tokens],
+                            rhs=moving[w][g][b].bitcast(FP8X4),
+                            rhs_scale=w_planes[PLANE_ROWS * g : P, w, b * BANK : (b + 1) * BANK],
+                            start=(g == 0),
+                            stop=(g == PASSES - 1),
+                        )
+                for (m, b), acc in zip(groups, accs):
                     columns = slice(b * BANK, (b + 1) * BANK)
-                    for m in range(TOKEN_TILES):
-                        acc = psum.tile([P, BANK], F32, tag="bank")
-                        for g in range(PASSES):
-                            tokens = slice(g * P, (g + 1) * P)
-                            nc.tensor.matmul_mx(
-                                out=acc[:],
-                                lhsT=x_codes[:, m, tokens].bitcast(FP8X4),
-                                lhsT_scale=x_planes[:, m, tokens],
-                                rhs=w_codes[w][h][:, g, columns].bitcast(FP8X4),
-                                rhs_scale=w_planes[PLANE_ROWS * g : P, w, h * HALF + b * BANK : h * HALF + (b + 1) * BANK],
-                                start=(g == 0),
-                                stop=(g == PASSES - 1),
-                            )
-                        if w < ROTATED:
-                            rotate(nc, scratch, acc, y_tiles[m][:, columns], cos_tab[:, m, :], sin_tab[:, m, :])
-                        else:
-                            nc.scalar.copy(out=y_tiles[m][:, columns], in_=acc[:])
+                    if w < ROTATED:
+                        rotate(nc, scratch, acc, y_tiles[m][:, columns], cos_tab[:, m, :], sin_tab[:, m, :])
+                    else:
+                        nc.scalar.copy(out=y_tiles[m][:, columns], in_=acc[:])
+                    last_tile = w == WEIGHTS - 1 and m == TOKEN_TILES - 1
+                    if last_tile and b == banks // 2 - 1:
+                        nc.sync.dma_start(out=outs[w][m][:, :HALF], in_=y_tiles[m][:, :HALF])
+                    if last_tile and b == banks - 1:
+                        nc.sync.dma_start(out=outs[w][m][:, HALF:], in_=y_tiles[m][:, HALF:])
+                    if w == WEIGHTS - 1 and not last_tile and b == banks - 1:
+                        nc.sync.dma_start(out=outs[w][m], in_=y_tiles[m][:])
+            if w < ROTATED:
                 for m in range(TOKEN_TILES):
-                    nc.sync.dma_start(out=outs[w][m][:, h * HALF : (h + 1) * HALF], in_=y_tiles[m][:])
+                    nc.sync.dma_start(out=outs[w][m], in_=y_tiles[m][:])

@@ -144,7 +144,7 @@ def tile_attention_pa_kernel(
 
         rounds_of = [
             [[(m, b)] for b in range(banks) for m in range(TOKEN_TILES)],
-            [[(m, b) for m in range(TOKEN_TILES)] for b in range(banks)],
+            [[(m, b) for b in range(banks)] for m in range(TOKEN_TILES)],
             [[(m, b)] for m in range(TOKEN_TILES) for b in range(banks)],
         ]
         for w in range(WEIGHTS):
@@ -176,6 +176,12 @@ def tile_attention_pa_kernel(
                         nc.sync.dma_start(out=outs[w][m][:, HALF:], in_=y_tiles[m][:, HALF:])
                     if w == WEIGHTS - 1 and not last_tile and b == banks - 1:
                         nc.sync.dma_start(out=outs[w][m], in_=y_tiles[m][:])
-            if w < ROTATED:
+                        if m == 0:
+                            nc.sync.dma_start(out=outs[1][TOKEN_TILES - 1], in_=late_k[:])
+                if w == 1 and groups[0][0] < TOKEN_TILES - 1:
+                    nc.sync.dma_start(out=outs[w][groups[0][0]], in_=y_tiles[groups[0][0]][:])
+                if w == 1 and groups[0][0] == TOKEN_TILES - 1:
+                    late_k = y_tiles[groups[0][0]]
+            if w == 0:
                 for m in range(TOKEN_TILES):
                     nc.sync.dma_start(out=outs[w][m], in_=y_tiles[m][:])

@@ -92,7 +92,11 @@ def tile_attention_pa_kernel(
         for w in range(WEIGHTS):
             load_scale_planes(nc, w_planes[:, w, :], w_scales[w])
             if w == 0:
-                for first, width in ((0, BANK), (BANK, BANK), (HALF, HALF)):
+                for g in range(PASSES):
+                    opening = keep.tile([P, BANK], U32, name="wq_opening_%d" % g, align_bytes=64)
+                    nc.sync.dma_start(out=opening[:].bitcast(I32), in_=w_words[w][:, g, :BANK])
+                    moving[w][g][0] = opening[:]
+                for first, width in ((BANK, BANK), (HALF, HALF)):
                     piece = keep.tile([P, PASSES, width], U32, name="wq_codes_%d" % first, align_bytes=64)
                     nc.sync.dma_start(out=piece[:].bitcast(I32), in_=w_words[w][:, :, first : first + width])
                     for g in range(PASSES):
@@ -143,7 +147,7 @@ def tile_attention_pa_kernel(
             )
 
         rounds_of = [
-            [[(m, b)] for b in range(banks) for m in range(TOKEN_TILES)],
+            [[(m, 0) for m in range(TOKEN_TILES)]] + [[(m, b)] for b in range(1, banks) for m in range(TOKEN_TILES)],
             [[(m, b) for b in range(banks)] for m in range(TOKEN_TILES)],
             [[(m, b)] for m in range(TOKEN_TILES) for b in range(banks)],
         ]

@@ -38,13 +38,13 @@ def load_scale_planes(nc, planes, scales):
     for quadrant in range(QUADRANTS):
         first = 32 * quadrant
         rows = slice(PLANE_ROWS * quadrant, PLANE_ROWS * (quadrant + 1))
-        nc.sync.dma_start(
-            out=planes[first : first + PASSES * PLANE_ROWS, :].bitcast(I32),
-            in_=scales[:, rows, :].bitcast(I32),
+        nc.gpsimd.dma_start(
+            out=planes[first : first + PASSES * PLANE_ROWS, :].bitcast(F32),
+            in_=scales[:, rows, :].bitcast(F32),
         )
 
 
-def rotate(nc, scratch, acc, y, cos_m, sin_m):
+def rotate(nc, adder, scratch, acc, y, cos_m, sin_m):
     by_head = [P, HEADS_PER_BANK, HEAD]
     by_pair = [P, HEADS_PER_BANK, PAIRS, 2]
     nc.vector.tensor_tensor(
@@ -60,7 +60,7 @@ def rotate(nc, scratch, acc, y, cos_m, sin_m):
         in1=sin_m.rearrange("p (j e) -> p j e", e=2).unsqueeze(1).to_broadcast(by_pair),
         op=MULT,
     )
-    nc.gpsimd.tensor_tensor(out=y, in0=y, in1=crossed[:], op=ADD)
+    adder.tensor_tensor(out=y, in0=y, in1=crossed[:], op=ADD)
 
 
 def tile_attention_pa_kernel(
@@ -77,6 +77,10 @@ def tile_attention_pa_kernel(
         keep = ctx.enter_context(tc.tile_pool(name="keep", bufs=1))
         scratch = ctx.enter_context(tc.tile_pool(name="scratch", bufs=6))
         psum = ctx.enter_context(tc.psum_pool(name="psum", bufs=8))
+        ctx.enter_context(tc.manual_schedule(engines={mybir.EngineType.Pool}))
+
+        identity = keep.tile([P, P], F32)
+        masks.make_identity(nc, identity[:])
 
         x_raw = keep.tile([P, TOKEN_TILES, FEATURES], BF16)
         table = keep.tile([P, TOKEN_TILES, HEAD], BF16)
@@ -96,7 +100,7 @@ def tile_attention_pa_kernel(
                     opening = keep.tile([P, BANK], U32, name="wq_opening_%d" % g, align_bytes=64)
                     nc.sync.dma_start(out=opening[:].bitcast(I32), in_=w_words[w][:, g, :BANK])
                     moving[w][g][0] = opening[:]
-                for first, width in ((BANK, BANK), (HALF, HALF)):
+                for first, width in ((BANK, BANK), (2 * BANK, BANK), (3 * BANK, BANK)):
                     piece = keep.tile([P, PASSES, width], U32, name="wq_codes_%d" % first, align_bytes=64)
                     nc.sync.dma_start(out=piece[:].bitcast(I32), in_=w_words[w][:, :, first : first + width])
                     for g in range(PASSES):
@@ -118,8 +122,6 @@ def tile_attention_pa_kernel(
         nc.scalar.mul(out=sin_pairs[:, :, 0:1], in_=table_pairs[:, :, 1:2], mul=-1.0)
         nc.scalar.copy(out=sin_pairs[:, :, 1:2], in_=table_pairs[:, :, 1:2])
 
-        identity = keep.tile([P, P], F32)
-        masks.make_identity(nc, identity[:])
         x_grouped = keep.tile([P, TOKEN_TILES, PASSES * P * PACK], BF16, align_bytes=64)
         x_codes = keep.tile([P, TOKEN_TILES, PASSES * P], U32, align_bytes=64)
         x_planes = keep.tile([P, TOKEN_TILES, PASSES * P], U8, align_bytes=64)
@@ -146,46 +148,56 @@ def tile_attention_pa_kernel(
                 out=x_codes[:, m, :].bitcast(FP8X4), scales=x_planes[:, m, :], in_=x_grouped[:, m, :]
             )
 
+        def whole_banks(m, some_banks):
+            return [(m, b * BANK, BANK) for b in some_banks]
+
+        last = TOKEN_TILES - 1
         rounds_of = [
-            [[(m, 0) for m in range(TOKEN_TILES)]] + [[(m, b)] for b in range(1, banks) for m in range(TOKEN_TILES)],
-            [[(m, b) for b in range(banks)] for m in range(TOKEN_TILES)],
-            [[(m, b)] for m in range(TOKEN_TILES) for b in range(banks)],
+            [[(m, 0, BANK) for m in range(last)], [(last, 0, BANK)]]
+            + [[(m, b * BANK, BANK)] for b in range(1, banks) for m in range(TOKEN_TILES)],
+            [whole_banks(m, range(banks)) for m in range(TOKEN_TILES)],
+            [whole_banks(0, range(banks))]
+            + [[group] for group in whole_banks(1, range(banks))]
+            + [[group] for group in whole_banks(last, range(banks - 1))]
+            + [[(last, FEATURES - BANK, BANK // 2)], [(last, FEATURES - BANK // 2, BANK // 2)]],
         ]
+        y_tiles = [
+            [keep.tile([P, FEATURES], F32, name="y_%d_%d" % (w, m)) for m in range(TOKEN_TILES)] for w in range(WEIGHTS)
+        ]
+        stores_after = {
+            (0, last, FEATURES): [(0, m, 0, FEATURES) for m in range(TOKEN_TILES)],
+            (1, 0, FEATURES): [(1, 0, 0, FEATURES)],
+            (1, 1, FEATURES): [(1, 1, 0, FEATURES)],
+            (2, 0, FEATURES): [(2, 0, 0, FEATURES)],
+            (2, 1, FEATURES): [(2, 1, 0, FEATURES), (1, last, 0, FEATURES)],
+            (2, last, HALF): [(2, last, 0, HALF)],
+            (2, last, HALF + BANK): [(2, last, HALF, HALF + BANK)],
+            (2, last, FEATURES - BANK // 2): [(2, last, FEATURES - BANK, FEATURES - BANK // 2)],
+            (2, last, FEATURES): [(2, last, FEATURES - BANK // 2, FEATURES)],
+        }
         for w in range(WEIGHTS):
-            y_tiles = [keep.tile([P, FEATURES], F32, name="y_%d_%d" % (w, m)) for m in range(TOKEN_TILES)]
             for groups in rounds_of[w]:
-                accs = [psum.tile([P, BANK], F32, tag="bank", name="acc") for group in groups]
+                accs = [psum.tile([P, width], F32, tag="bank", name="acc") for (m, first, width) in groups]
                 for g in range(PASSES):
                     tokens = slice(g * P, (g + 1) * P)
-                    for (m, b), acc in zip(groups, accs):
+                    for (m, first, width), acc in zip(groups, accs):
+                        inside = first % BANK
                         nc.tensor.matmul_mx(
                             out=acc[:],
                             lhsT=x_codes[:, m, tokens].bitcast(FP8X4),
                             lhsT_scale=x_planes[:, m, tokens],
-                            rhs=moving[w][g][b].bitcast(FP8X4),
-                            rhs_scale=w_planes[PLANE_ROWS * g : P, w, b * BANK : (b + 1) * BANK],
+                            rhs=moving[w][g][first // BANK][:, inside : inside + width].bitcast(FP8X4),
+                            rhs_scale=w_planes[PLANE_ROWS * g : P, w, first : first + width],
                             start=(g == 0),
                             stop=(g == PASSES - 1),
                         )
-                for (m, b), acc in zip(groups, accs):
-                    columns = slice(b * BANK, (b + 1) * BANK)
+                for (m, first, width), acc in zip(groups, accs):
+                    columns = slice(first, first + width)
                     if w < ROTATED:
-                        rotate(nc, scratch, acc, y_tiles[m][:, columns], cos_tab[:, m, :], sin_tab[:, m, :])
+                        idle_next = (w == 0 and first == FEATURES - BANK) or (w == 1 and m == last)
+                        adder = nc.vector if idle_next else nc.gpsimd
+                        rotate(nc, adder, scratch, acc, y_tiles[w][m][:, columns], cos_tab[:, m, :], sin_tab[:, m, :])
                     else:
-                        nc.scalar.copy(out=y_tiles[m][:, columns], in_=acc[:])
-                    last_tile = w == WEIGHTS - 1 and m == TOKEN_TILES - 1
-                    if last_tile and b == banks // 2 - 1:
-                        nc.sync.dma_start(out=outs[w][m][:, :HALF], in_=y_tiles[m][:, :HALF])
-                    if last_tile and b == banks - 1:
-                        nc.sync.dma_start(out=outs[w][m][:, HALF:], in_=y_tiles[m][:, HALF:])
-                    if w == WEIGHTS - 1 and not last_tile and b == banks - 1:
-                        nc.sync.dma_start(out=outs[w][m], in_=y_tiles[m][:])
-                        if m == 0:
-                            nc.sync.dma_start(out=outs[1][TOKEN_TILES - 1], in_=late_k[:])
-                if w == 1 and groups[0][0] < TOKEN_TILES - 1:
-                    nc.sync.dma_start(out=outs[w][groups[0][0]], in_=y_tiles[groups[0][0]][:])
-                if w == 1 and groups[0][0] == TOKEN_TILES - 1:
-                    late_k = y_tiles[groups[0][0]]
-            if w == 0:
-                for m in range(TOKEN_TILES):
-                    nc.sync.dma_start(out=outs[w][m], in_=y_tiles[m][:])
+                        nc.scalar.copy(out=y_tiles[w][m][:, columns], in_=acc[:])
+                    for (sw, sm, begin, end) in stores_after.get((w, m, first + width), []):
+                        nc.sync.dma_start(out=outs[sw][sm][:, begin:end], in_=y_tiles[sw][sm][:, begin:end])

@@ -84,9 +84,13 @@ def tile_attention_pa_kernel(
 
         x_raw = keep.tile([P, TOKEN_TILES, FEATURES], BF16)
         table = keep.tile([P, TOKEN_TILES, HEAD], BF16)
-        w_planes = keep.tile([P, WEIGHTS, FEATURES], U8, align_bytes=64)
+        w_planes = [keep.tile([P, FEATURES], U8, name="w_planes_%d" % w, align_bytes=64) for w in range(WEIGHTS)]
 
-        nc.vector.memset(w_planes[:].rearrange("p w n -> p (w n)").bitcast(I32), 0)
+        for planes in w_planes:
+            nc.vector.memset(planes[:].bitcast(I32), 0)
+        signs = keep.tile([P, 2], F32)
+        nc.vector.memset(signs[:, 0:1], -1.0)
+        nc.vector.memset(signs[:, 1:2], 1.0)
 
         nc.scalar.dma_start(out=table[:], in_=freqs_cis.rearrange("(m p) j e -> p m (j e)", p=P))
         for m in range(TOKEN_TILES):
@@ -94,7 +98,7 @@ def tile_attention_pa_kernel(
 
         moving = [[[None] * banks for g in range(PASSES)] for w in range(WEIGHTS)]
         for w in range(WEIGHTS):
-            load_scale_planes(nc, w_planes[:, w, :], w_scales[w])
+            load_scale_planes(nc, w_planes[w][:], w_scales[w])
             if w == 0:
                 for g in range(PASSES):
                     opening = keep.tile([P, BANK], U32, name="wq_opening_%d" % g, align_bytes=64)
@@ -112,15 +116,6 @@ def tile_attention_pa_kernel(
                     nc.sync.dma_start(out=rows[:].bitcast(I32), in_=w_words[w][:, g, :])
                     for b in range(banks):
                         moving[w][g][b] = rows[:, b * BANK : (b + 1) * BANK]
-
-        cos_tab = keep.tile([P, TOKEN_TILES, HEAD], F32)
-        sin_tab = keep.tile([P, TOKEN_TILES, HEAD], F32)
-        table_pairs = table[:].rearrange("p m (j e) -> p (m j) e", e=2)
-        cos_pairs = cos_tab[:].rearrange("p m (j e) -> p (m j) e", e=2)
-        sin_pairs = sin_tab[:].rearrange("p m (j e) -> p (m j) e", e=2)
-        nc.scalar.copy(out=cos_pairs, in_=table_pairs[:, :, 0:1].to_broadcast([P, TOKEN_TILES * PAIRS, 2]))
-        nc.scalar.mul(out=sin_pairs[:, :, 0:1], in_=table_pairs[:, :, 1:2], mul=-1.0)
-        nc.scalar.copy(out=sin_pairs[:, :, 1:2], in_=table_pairs[:, :, 1:2])
 
         x_grouped = keep.tile([P, TOKEN_TILES, PASSES * P * PACK], BF16, align_bytes=64)
         x_codes = keep.tile([P, TOKEN_TILES, PASSES * P], U32, align_bytes=64)
@@ -147,6 +142,19 @@ def tile_attention_pa_kernel(
             nc.vector.quantize_mx(
                 out=x_codes[:, m, :].bitcast(FP8X4), scales=x_planes[:, m, :], in_=x_grouped[:, m, :]
             )
+
+        cos_tab = keep.tile([P, TOKEN_TILES, HEAD], F32)
+        sin_tab = keep.tile([P, TOKEN_TILES, HEAD], F32)
+        table_pairs = table[:].rearrange("p m (j e) -> p (m j) e", e=2)
+        cos_pairs = cos_tab[:].rearrange("p m (j e) -> p (m j) e", e=2)
+        sin_pairs = sin_tab[:].rearrange("p m (j e) -> p (m j) e", e=2)
+        nc.scalar.copy(out=cos_pairs, in_=table_pairs[:, :, 0:1].to_broadcast([P, TOKEN_TILES * PAIRS, 2]))
+        nc.vector.tensor_tensor(
+            out=sin_pairs,
+            in0=table_pairs[:, :, 1:2].to_broadcast([P, TOKEN_TILES * PAIRS, 2]),
+            in1=signs[:].unsqueeze(1).to_broadcast([P, TOKEN_TILES * PAIRS, 2]),
+            op=MULT,
+        )
 
         def whole_banks(m, some_banks):
             return [(m, b * BANK, BANK) for b in some_banks]
@@ -187,7 +195,7 @@ def tile_attention_pa_kernel(
                             lhsT=x_codes[:, m, tokens].bitcast(FP8X4),
                             lhsT_scale=x_planes[:, m, tokens],
                             rhs=moving[w][g][first // BANK][:, inside : inside + width].bitcast(FP8X4),
-                            rhs_scale=w_planes[PLANE_ROWS * g : P, w, first : first + width],
+                            rhs_scale=w_planes[w][PLANE_ROWS * g : P, first : first + width],
                             start=(g == 0),
                             stop=(g == PASSES - 1),
                         )

from contextlib import ExitStack

import concourse.masks as masks
import concourse.mybir as mybir

F32 = mybir.dt.float32
BF16 = mybir.dt.bfloat16
I32 = mybir.dt.int32
U32 = mybir.dt.uint32
U8 = mybir.dt.uint8
FP8X4 = mybir.dt.float8_e4m3fn_x4
MULT = mybir.AluOpType.mult
ADD = mybir.AluOpType.add

P = 128
TOKENS = 384
FEATURES = 2048
HEAD = 128
PAIRS = HEAD // 2
TOKEN_TILES = TOKENS // P
PACK = 4
K_PASS = P * PACK
PASSES = FEATURES // K_PASS
BANK = 512
HALF = 1024
BANKS_PER_HALF = HALF // BANK
HALVES = FEATURES // HALF
HEADS_PER_BANK = BANK // HEAD
WEIGHTS = 3
ROTATED = 2
QUADRANTS = 4
PLANE_ROWS = 4

FLOPS = 2 * TOKENS * FEATURES * WEIGHTS * FEATURES


def load_scale_planes(nc, planes, scales):
    for quadrant in range(QUADRANTS):
        first = 32 * quadrant
        rows = slice(PLANE_ROWS * quadrant, PLANE_ROWS * (quadrant + 1))
        nc.gpsimd.dma_start(
            out=planes[first : first + PASSES * PLANE_ROWS, :].bitcast(F32),
            in_=scales[:, rows, :].bitcast(F32),
        )


def rotate(nc, adder, scratch, acc, y, cos_m, sin_m):
    by_head = [P, HEADS_PER_BANK, HEAD]
    by_pair = [P, HEADS_PER_BANK, PAIRS, 2]
    nc.vector.tensor_tensor(
        out=y.rearrange("p (h d) -> p h d", d=HEAD),
        in0=acc[:].rearrange("p (h d) -> p h d", d=HEAD),
        in1=cos_m.unsqueeze(1).to_broadcast(by_head),
        op=MULT,
    )
    crossed = scratch.tile([P, BANK], F32)
    nc.vector.tensor_tensor(
        out=crossed[:].rearrange("p (h j e) -> p h j e", j=PAIRS, e=2),
        in0=acc[:].rearrange("p (h j e) -> p h j e", j=PAIRS, e=2)[:, :, :, ::-1],
        in1=sin_m.rearrange("p (j e) -> p j e", e=2).unsqueeze(1).to_broadcast(by_pair),
        op=MULT,
    )
    adder.tensor_tensor(out=y, in0=y, in1=crossed[:], op=ADD)


def tile_attention_pa_kernel(
    tc, x, freqs_cis, wq_words, wq_scales, wk_words, wk_scales, wv_words, wv_scales, out_0, out_1, out_2
):
    nc = tc.nc
    x_tiles = x.rearrange("b (m p) k -> (b m) p k", p=P)
    w_words = [w.rearrange("g p n t -> p g (n t)").bitcast(I32) for w in (wq_words, wk_words, wv_words)]
    w_scales = [wq_scales, wk_scales, wv_scales]
    outs = [o.rearrange("b (m p) h d -> (b m) p (h d)", p=P) for o in (out_0, out_1, out_2)]
    banks = FEATURES // BANK

    with ExitStack() as ctx:
        keep = ctx.enter_context(tc.tile_pool(name="keep", bufs=1))
        scratch = ctx.enter_context(tc.tile_pool(name="scratch", bufs=6))
        psum = ctx.enter_context(tc.psum_pool(name="psum", bufs=8))
        ctx.enter_context(tc.manual_schedule(engines={mybir.EngineType.Pool}))

        identity = keep.tile([P, P], F32)
        masks.make_identity(nc, identity[:])

        x_raw = keep.tile([P, TOKEN_TILES, FEATURES], BF16)
        table = keep.tile([P, TOKEN_TILES, HEAD], BF16)
        w_planes = [keep.tile([P, FEATURES], U8, name="w_planes_%d" % w, align_bytes=64) for w in range(WEIGHTS)]

        for planes in w_planes:
            nc.vector.memset(planes[:].bitcast(I32), 0)
        signs = keep.tile([P, 2], F32)
        nc.vector.memset(signs[:, 0:1], -1.0)
        nc.vector.memset(signs[:, 1:2], 1.0)

        nc.scalar.dma_start(out=table[:], in_=freqs_cis.rearrange("(m p) j e -> p m (j e)", p=P))
        for m in range(TOKEN_TILES):
            nc.sync.dma_start(out=x_raw[:, m, :], in_=x_tiles[m])

        moving = [[[None] * banks for g in range(PASSES)] for w in range(WEIGHTS)]
        for w in range(WEIGHTS):
            load_scale_planes(nc, w_planes[w][:], w_scales[w])
            if w == 0:
                for g in range(PASSES):
                    opening = keep.tile([P, BANK], U32, name="wq_opening_%d" % g, align_bytes=64)
                    nc.sync.dma_start(out=opening[:].bitcast(I32), in_=w_words[w][:, g, :BANK])
                    moving[w][g][0] = opening[:]
                for first, width in ((BANK, BANK), (2 * BANK, BANK), (3 * BANK, BANK)):
                    piece = keep.tile([P, PASSES, width], U32, name="wq_codes_%d" % first, align_bytes=64)
                    nc.sync.dma_start(out=piece[:].bitcast(I32), in_=w_words[w][:, :, first : first + width])
                    for g in range(PASSES):
                        for b in range(width // BANK):
                            moving[w][g][first // BANK + b] = piece[:, g, b * BANK : (b + 1) * BANK]
            else:
                for g in range(PASSES):
                    rows = keep.tile([P, FEATURES], U32, name="w_codes_%d_%d" % (w, g), align_bytes=64)
                    nc.sync.dma_start(out=rows[:].bitcast(I32), in_=w_words[w][:, g, :])
                    for b in range(banks):
                        moving[w][g][b] = rows[:, b * BANK : (b + 1) * BANK]

        x_grouped = keep.tile([P, TOKEN_TILES, PASSES * P * PACK], BF16, align_bytes=64)
        x_codes = keep.tile([P, TOKEN_TILES, PASSES * P], U32, align_bytes=64)
        x_planes = keep.tile([P, TOKEN_TILES, PASSES * P], U8, align_bytes=64)
        passes_per_bank = BANK // (2 * P)
        for m in range(TOKEN_TILES):
            x_words = x_raw[:, m, :].bitcast(F32)
            grouped_words = x_grouped[:, m, :].bitcast(F32)
            for bank in range(PASSES // passes_per_bank):
                turned = psum.tile([P, passes_per_bank, 2, P], F32, tag="bank")
                for i in range(passes_per_bank):
                    g = bank * passes_per_bank + i
                    for u in range(2):
                        nc.tensor.transpose(
                            turned[:, i, u, :], x_words[:, 2 * P * g + u : 2 * P * (g + 1) : 2], identity[:]
                        )
                copy = nc.vector.tensor_copy if bank % 2 == 0 else nc.scalar.copy
                copy(
                    out=grouped_words[:, bank * BANK : (bank + 1) * BANK].rearrange(
                        "p (i r u) -> p i r u", i=passes_per_bank, u=2
                    ),
                    in_=turned[:].rearrange("p i u r -> p i r u"),
                )
            nc.vector.quantize_mx(
                out=x_codes[:, m, :].bitcast(FP8X4), scales=x_planes[:, m, :], in_=x_grouped[:, m, :]
            )

        cos_tab = keep.tile([P, TOKEN_TILES, HEAD], F32)
        sin_tab = keep.tile([P, TOKEN_TILES, HEAD], F32)
        table_pairs = table[:].rearrange("p m (j e) -> p (m j) e", e=2)
        cos_pairs = cos_tab[:].rearrange("p m (j e) -> p (m j) e", e=2)
        sin_pairs = sin_tab[:].rearrange("p m (j e) -> p (m j) e", e=2)
        nc.scalar.copy(out=cos_pairs, in_=table_pairs[:, :, 0:1].to_broadcast([P, TOKEN_TILES * PAIRS, 2]))
        nc.vector.tensor_tensor(
            out=sin_pairs,
            in0=table_pairs[:, :, 1:2].to_broadcast([P, TOKEN_TILES * PAIRS, 2]),
            in1=signs[:].unsqueeze(1).to_broadcast([P, TOKEN_TILES * PAIRS, 2]),
            op=MULT,
        )

        def whole_banks(m, some_banks):
            return [(m, b * BANK, BANK) for b in some_banks]

        last = TOKEN_TILES - 1
        rounds_of = [
            [[(m, 0, BANK) for m in range(last)], [(last, 0, BANK)]]
            + [[(m, b * BANK, BANK)] for b in range(1, banks) for m in range(TOKEN_TILES)],
            [whole_banks(m, range(banks)) for m in range(TOKEN_TILES)],
            [whole_banks(0, range(banks))]
            + [[group] for group in whole_banks(1, range(banks))]
            + [[group] for group in whole_banks(last, range(banks - 1))]
            + [[(last, FEATURES - BANK, BANK // 2)], [(last, FEATURES - BANK // 2, BANK // 2)]],
        ]
        y_tiles = [
            [keep.tile([P, FEATURES], F32, name="y_%d_%d" % (w, m)) for m in range(TOKEN_TILES)] for w in range(WEIGHTS)
        ]
        stores_after = {
            (0, last, FEATURES): [(0, m, 0, FEATURES) for m in range(TOKEN_TILES)],
            (1, 0, FEATURES): [(1, 0, 0, FEATURES)],
            (1, 1, FEATURES): [(1, 1, 0, FEATURES)],
            (2, 0, FEATURES): [(2, 0, 0, FEATURES)],
            (2, 1, FEATURES): [(2, 1, 0, FEATURES), (1, last, 0, FEATURES)],
            (2, last, HALF): [(2, last, 0, HALF)],
            (2, last, HALF + BANK): [(2, last, HALF, HALF + BANK)],
            (2, last, FEATURES - BANK // 2): [(2, last, FEATURES - BANK, FEATURES - BANK // 2)],
            (2, last, FEATURES): [(2, last, FEATURES - BANK // 2, FEATURES)],
        }
        for w in range(WEIGHTS):
            for groups in rounds_of[w]:
                accs = [psum.tile([P, width], F32, tag="bank", name="acc") for (m, first, width) in groups]
                for g in range(PASSES):
                    tokens = slice(g * P, (g + 1) * P)
                    for (m, first, width), acc in zip(groups, accs):
                        inside = first % BANK
                        nc.tensor.matmul_mx(
                            out=acc[:],
                            lhsT=x_codes[:, m, tokens].bitcast(FP8X4),
                            lhsT_scale=x_planes[:, m, tokens],
                            rhs=moving[w][g][first // BANK][:, inside : inside + width].bitcast(FP8X4),
                            rhs_scale=w_planes[w][PLANE_ROWS * g : P, first : first + width],
                            start=(g == 0),
                            stop=(g == PASSES - 1),
                        )
                for (m, first, width), acc in zip(groups, accs):
                    columns = slice(first, first + width)
                    if w < ROTATED:
                        idle_next = (w == 0 and first == FEATURES - BANK) or (w == 1 and m == last)
                        adder = nc.vector if idle_next else nc.gpsimd
                        rotate(nc, adder, scratch, acc, y_tiles[w][m][:, columns], cos_tab[:, m, :], sin_tab[:, m, :])
                    else:
                        nc.scalar.copy(out=y_tiles[w][m][:, columns], in_=acc[:])
                    for (sw, sm, begin, end) in stores_after.get((w, m, first + width), []):
                        nc.sync.dma_start(out=outs[sw][sm][:, begin:end], in_=y_tiles[sw][sm][:, begin:end])
